import numpy as np
import ml_dtypes


def mxq(x, axis, fmt="e4m3"):
    dtype, down = {"e4m3": (ml_dtypes.float8_e4m3fn, 7), "e5m2": (ml_dtypes.float8_e5m2, 14)}[fmt]
    v = np.moveaxis(np.asarray(x, np.float32).astype(ml_dtypes.bfloat16).astype(np.float64), axis, -1)
    blocks = v.reshape(v.shape[:-1] + (-1, 32))
    amax = np.abs(blocks).max(-1, keepdims=True)
    byte = np.maximum(np.where(amax > 0, np.frexp(amax)[1] - 1 + 127, 0) - down, 1)
    scale = np.exp2(byte - 127.0)
    codes = (blocks / scale).astype(np.float32).astype(dtype).astype(np.float64)
    return np.moveaxis((codes * scale).reshape(v.shape), -1, axis)


WIDE = False


def mx_kscale(k):
    if not WIDE:
        return np.ones(k)
    levels = np.array([10, -10, 5, -5, 0])
    a = np.random.permutation(np.resize(levels, k // 512 * 4)).reshape(k // 512, 4)
    idx = np.arange(k)
    return np.exp2(a[idx // 512, idx % 128 // 32])


BF16 = ml_dtypes.bfloat16


def bf(x):
    return np.asarray(x, np.float32).astype(BF16)


def f64(x):
    return np.asarray(x).astype(np.float64)


BATCH, IN_F, OUT_F, RANK, N_ADAPTERS = 1024, 16384, 128, 128, 8
SEG = BATCH // N_ADAPTERS
LORA_GAIN = 2.0


def setup_inputs():
    s = mx_kscale(IN_F)
    return {"x": bf(np.random.standard_normal((BATCH, IN_F)) * s),
            "h_lora": bf(np.random.standard_normal((N_ADAPTERS, SEG, RANK))),
            "lora_B": bf(np.random.standard_normal((N_ADAPTERS, RANK, OUT_F)) * 0.5 / np.sqrt(RANK)),
            "M": bf(np.random.standard_normal((IN_F, OUT_F)) / np.sqrt(IN_F) / s[:, None])}


def reference(x, h_lora, lora_B, M):
    y = (f64(h_lora) @ f64(lora_B)) * LORA_GAIN
    y = y.reshape(BATCH, OUT_F)
    return y + (mxq(f64(x), 1, "e4m3") @ mxq(f64(M), 0, "e4m3"))

@@ -1,0 +1,200 @@
+from contextlib import ExitStack
+
+import concourse.mybir as mybir
+from concourse.masks import make_identity
+
+BF16 = mybir.dt.bfloat16
+F32 = mybir.dt.float32
+U32 = mybir.dt.uint32
+U8 = mybir.dt.uint8
+FP8X4 = mybir.dt.float8_e4m3fn_x4
+ADD = mybir.AluOpType.add
+
+P = 128
+BATCH, IN_F, OUT_F, RANK, N_ADAPTERS = 1024, 16384, 128, 128, 8
+LORA_GAIN = 2.0
+
+PACK = 4
+K_PASS = P * PACK
+CHUNK_K = 4096
+PASSES = CHUNK_K // K_PASS
+K_STEPS = IN_F // CHUNK_K
+ROW_TILES = BATCH // P
+N_CHUNKS = K_STEPS * ROW_TILES
+BANK_PASSES = 2
+CHUNK_BANKS = PASSES // BANK_PASSES
+QUANT_COLS = 2048
+
+LOADS_AHEAD = 6
+QUANTISE_LAG = 1
+MULTIPLY_LAG = 2
+M_LEAD = PASSES - MULTIPLY_LAG
+M_LOAD_AT = PASSES - M_LEAD
+
+FLOPS = 2 * BATCH * IN_F * OUT_F + 2 * BATCH * RANK * OUT_F
+
+
+def tile_lorasequential_pa_k_kernel(tc, x, h_lora, lora_B, M, out):
+    nc = tc.nc
+    with ExitStack() as ctx:
+        ctx.enter_context(tc.manual_schedule())
+        const = ctx.enter_context(tc.tile_pool(name="const", bufs=1))
+        x_pool = ctx.enter_context(tc.tile_pool(name="x", bufs=LOADS_AHEAD + 1))
+        x_mx_pool = ctx.enter_context(tc.tile_pool(name="x_mx", bufs=3))
+        m_raw_pool = ctx.enter_context(tc.tile_pool(name="m_raw", bufs=2))
+        m_grouped_pool = ctx.enter_context(tc.tile_pool(name="m_grouped", bufs=3))
+        m_mx_pool = ctx.enter_context(tc.tile_pool(name="m_mx", bufs=2))
+        result_pool = ctx.enter_context(tc.tile_pool(name="result", bufs=4))
+        psum_t = ctx.enter_context(tc.psum_pool(name="psum_t", bufs=6))
+        psum_acc = ctx.enter_context(tc.psum_pool(name="psum_acc", bufs=2))
+
+        ident_f32 = const.tile([P, P], F32)
+        make_identity(nc, ident_f32[:])
+        ident_bf16 = const.tile([P, P], BF16)
+        make_identity(nc, ident_bf16[:])
+
+        x_raw = {}
+        x_grouped = {}
+        x_codes = {}
+        x_scales = {}
+        m_raw = {}
+        m_grouped = {}
+        m_codes = {}
+        m_scales = {}
+
+        def load_m(step):
+            raw = m_raw_pool.tile([P, PASSES, PACK, OUT_F], BF16, name="m_raw")
+            m_rows = M[step * CHUNK_K : (step + 1) * CHUNK_K, :]
+            nc.sync.dma_start(
+                out=raw[:].rearrange("p g (u e) o -> p g u e o", u=2),
+                in_=m_rows.rearrange("(g u p e) o -> p g u e o", u=2, p=P, e=2),
+            )
+            m_raw[step] = raw
+
+        def load_x(chunk):
+            step, row_tile = divmod(chunk, ROW_TILES)
+            if row_tile == M_LOAD_AT and step + 1 < K_STEPS:
+                load_m(step + 1)
+            raw = x_pool.tile([P, CHUNK_K], BF16, name="x_raw")
+            nc.sync.dma_start(
+                out=raw[:],
+                in_=x[row_tile * P : (row_tile + 1) * P, step * CHUNK_K : (step + 1) * CHUNK_K],
+            )
+            x_raw[chunk] = raw
+
+        def regroup_m(j):
+            step, g = divmod(j, PASSES)
+            grouped = m_grouped_pool.tile([P, OUT_F, PACK], BF16, name="m_grouped", align_bytes=64)
+            nc.vector.tensor_copy(out=grouped[:], in_=m_raw[step][:, g, :, :].rearrange("p t o -> p o t"))
+            m_grouped[j] = grouped
+
+        def quantise_m(j):
+            step, g = divmod(j, PASSES)
+            if g == 0:
+                m_codes[step] = m_mx_pool.tile([P, PASSES * OUT_F], U32, name="m_codes", align_bytes=64)
+                m_scales[step] = m_mx_pool.tile([P, PASSES * OUT_F], U8, name="m_scales", align_bytes=64)
+            cols = slice(g * OUT_F, (g + 1) * OUT_F)
+            nc.vector.quantize_mx(
+                out=m_codes[step][:, cols].bitcast(FP8X4),
+                scales=m_scales[step][:, cols],
+                in_=m_grouped[j][:].rearrange("p o t -> p (o t)"),
+            )
+
+        def transpose_x(chunk):
+            words = x_raw[chunk][:].bitcast(F32)
+            grouped = x_mx_pool.tile([P, PASSES * P * PACK], BF16, name="x_grouped", align_bytes=64)
+            grouped_words = grouped[:].bitcast(F32)
+            bank_words = BANK_PASSES * P * 2
+            for bank in range(CHUNK_BANKS):
+                xt = psum_t.tile([P, BANK_PASSES, 2, P], F32, name="xt", tag="bank")
+                for g in range(BANK_PASSES):
+                    for u in range(2):
+                        first = ((bank * BANK_PASSES + g) * 2 + u) * P
+                        nc.tensor.transpose(xt[:, g, u, :], words[:, first : first + P], ident_f32[:])
+                nc.scalar.copy(
+                    out=grouped_words[:, bank * bank_words : (bank + 1) * bank_words].rearrange(
+                        "p (g r u) -> p g r u", g=BANK_PASSES, u=2
+                    ),
+                    in_=xt[:].rearrange("p g u r -> p g r u"),
+                )
+            x_grouped[chunk] = grouped
+
+        def quantise_x(chunk):
+            codes = x_mx_pool.tile([P, PASSES * P], U32, name="x_codes", align_bytes=64)
+            scales = x_mx_pool.tile([P, PASSES * P], U8, name="x_scales", align_bytes=64)
+            for first in range(0, PASSES * P * PACK, QUANT_COLS):
+                cols = slice(first // PACK, (first + QUANT_COLS) // PACK)
+                nc.vector.quantize_mx(
+                    out=codes[:, cols].bitcast(FP8X4),
+                    scales=scales[:, cols],
+                    in_=x_grouped[chunk][:, first : first + QUANT_COLS],
+                )
+            x_codes[chunk] = codes
+            x_scales[chunk] = scales
+
+        def multiply(chunk):
+            step, row_tile = divmod(chunk, ROW_TILES)
+            acc = psum_acc.tile([P, OUT_F], F32, name="acc")
+            for g in range(PASSES):
+                rows = slice(g * P, (g + 1) * P)
+                outputs = slice(g * OUT_F, (g + 1) * OUT_F)
+                nc.tensor.matmul_mx(
+                    out=acc[:],
+                    lhsT=x_codes[chunk][:, rows].bitcast(FP8X4),
+                    lhsT_scale=x_scales[chunk][:, rows],
+                    rhs=m_codes[step][:, outputs].bitcast(FP8X4),
+                    rhs_scale=m_scales[step][:, outputs],
+                    start=(g == 0),
+                    stop=(g == PASSES - 1),
+                )
+            if step < K_STEPS - 1:
+                nc.vector.tensor_tensor(out=sums[:, row_tile, :], in0=acc[:], in1=sums[:, row_tile, :], op=ADD)
+            else:
+                result = result_pool.tile([P, OUT_F], F32, name="result")
+                nc.vector.tensor_tensor(out=result[:], in0=acc[:], in1=sums[:, row_tile, :], op=ADD)
+                nc.sync.dma_start(out=out[row_tile * P : (row_tile + 1) * P, :], in_=result[:])
+
+        load_m(0)
+        h_sb = const.tile([P, N_ADAPTERS, RANK], BF16)
+        nc.sync.dma_start(out=h_sb[:], in_=h_lora.rearrange("g b r -> b g r"))
+        b_sb = const.tile([P, N_ADAPTERS, OUT_F], BF16)
+        nc.sync.dma_start(out=b_sb[:], in_=lora_B.rearrange("g r o -> r g o"))
+        for chunk in range(LOADS_AHEAD):
+            load_x(chunk)
+
+        for j in range(PASSES):
+            regroup_m(j)
+            if j > 0:
+                quantise_m(j - 1)
+        quantise_m(PASSES - 1)
+
+        sums = const.tile([P, ROW_TILES, OUT_F], F32)
+        hT_ps = psum_t.tile([P, N_ADAPTERS, P], BF16, name="hT_ps", tag="bank")
+        for g in range(N_ADAPTERS):
+            nc.tensor.transpose(hT_ps[:, g, :], h_sb[:, g, :], ident_bf16[:])
+        hT_sb = const.tile([P, N_ADAPTERS, P], BF16)
+        nc.scalar.copy(out=hT_sb[:], in_=hT_ps[:])
+        bank_groups = 4
+        for first in range(0, N_ADAPTERS, bank_groups):
+            y_ps = psum_t.tile([P, bank_groups, OUT_F], F32, name="y_ps", tag="bank")
+            for g in range(bank_groups):
+                nc.tensor.matmul(
+                    y_ps[:, g, :], lhsT=hT_sb[:, first + g, :], rhs=b_sb[:, first + g, :], start=True, stop=True
+                )
+            nc.scalar.mul(out=sums[:, first : first + bank_groups, :], in_=y_ps[:], mul=LORA_GAIN)
+
+        for i in range(N_CHUNKS + MULTIPLY_LAG):
+            if i + LOADS_AHEAD < N_CHUNKS:
+                load_x(i + LOADS_AHEAD)
+            if i < N_CHUNKS:
+                transpose_x(i)
+            m_pass = i + M_LEAD
+            prepare_m = PASSES <= m_pass < K_STEPS * PASSES
+            if prepare_m:
+                regroup_m(m_pass)
+            if 0 <= i - QUANTISE_LAG < N_CHUNKS:
+                quantise_x(i - QUANTISE_LAG)
+            if prepare_m:
+                quantise_m(m_pass)
+            if i >= MULTIPLY_LAG:
+                multiply(i - MULTIPLY_LAG)

@@ -23,7 +23,7 @@ ROW_TILES = BATCH // P
 N_CHUNKS = K_STEPS * ROW_TILES
 BANK_PASSES = 2
 CHUNK_BANKS = PASSES // BANK_PASSES
-QUANT_COLS = 2048
+BANK_COLS = BANK_PASSES * P * PACK
 
 LOADS_AHEAD = 6
 QUANTISE_LAG = 1
@@ -76,10 +76,11 @@ def tile_lorasequential_pa_k_kernel(tc, x, h_lora, lora_B, M, out):
             if row_tile == M_LOAD_AT and step + 1 < K_STEPS:
                 load_m(step + 1)
             raw = x_pool.tile([P, CHUNK_K], BF16, name="x_raw")
-            nc.sync.dma_start(
-                out=raw[:],
-                in_=x[row_tile * P : (row_tile + 1) * P, step * CHUNK_K : (step + 1) * CHUNK_K],
-            )
+            x_rows = x[row_tile * P : (row_tile + 1) * P, step * CHUNK_K : (step + 1) * CHUNK_K]
+            pieces = CHUNK_BANKS if chunk == N_CHUNKS - 1 else 1
+            piece_k = CHUNK_K // pieces
+            for first in range(0, CHUNK_K, piece_k):
+                nc.sync.dma_start(out=raw[:, first : first + piece_k], in_=x_rows[:, first : first + piece_k])
             x_raw[chunk] = raw
 
         def regroup_m(j):
@@ -104,7 +105,7 @@ def tile_lorasequential_pa_k_kernel(tc, x, h_lora, lora_B, M, out):
             words = x_raw[chunk][:].bitcast(F32)
             grouped = x_mx_pool.tile([P, PASSES * P * PACK], BF16, name="x_grouped", align_bytes=64)
             grouped_words = grouped[:].bitcast(F32)
-            bank_words = BANK_PASSES * P * 2
+            bank_words = BANK_COLS // 2
             for bank in range(CHUNK_BANKS):
                 xt = psum_t.tile([P, BANK_PASSES, 2, P], F32, name="xt", tag="bank")
                 for g in range(BANK_PASSES):
@@ -122,12 +123,12 @@ def tile_lorasequential_pa_k_kernel(tc, x, h_lora, lora_B, M, out):
         def quantise_x(chunk):
             codes = x_mx_pool.tile([P, PASSES * P], U32, name="x_codes", align_bytes=64)
             scales = x_mx_pool.tile([P, PASSES * P], U8, name="x_scales", align_bytes=64)
-            for first in range(0, PASSES * P * PACK, QUANT_COLS):
-                cols = slice(first // PACK, (first + QUANT_COLS) // PACK)
+            for first in range(0, CHUNK_BANKS * BANK_COLS, BANK_COLS):
+                cols = slice(first // PACK, (first + BANK_COLS) // PACK)
                 nc.vector.quantize_mx(
                     out=codes[:, cols].bitcast(FP8X4),
                     scales=scales[:, cols],
-                    in_=x_grouped[chunk][:, first : first + QUANT_COLS],
+                    in_=x_grouped[chunk][:, first : first + BANK_COLS],
                 )
             x_codes[chunk] = codes
             x_scales[chunk] = scales
@@ -186,6 +187,8 @@ def tile_lorasequential_pa_k_kernel(tc, x, h_lora, lora_B, M, out):
         for i in range(N_CHUNKS + MULTIPLY_LAG):
             if i + LOADS_AHEAD < N_CHUNKS:
                 load_x(i + LOADS_AHEAD)
+            if i >= MULTIPLY_LAG:
+                multiply(i - MULTIPLY_LAG)
             if i < N_CHUNKS:
                 transpose_x(i)
             m_pass = i + M_LEAD
@@ -196,5 +199,3 @@ def tile_lorasequential_pa_k_kernel(tc, x, h_lora, lora_B, M, out):
                 quantise_x(i - QUANTISE_LAG)
             if prepare_m:
                 quantise_m(m_pass)
-            if i >= MULTIPLY_LAG:
-                multiply(i - MULTIPLY_LAG)

@@ -23,13 +23,14 @@ ROW_TILES = BATCH // P
 N_CHUNKS = K_STEPS * ROW_TILES
 BANK_PASSES = 2
 CHUNK_BANKS = PASSES // BANK_PASSES
-BANK_COLS = BANK_PASSES * P * PACK
+QUANT_COLS = 2048
 
 LOADS_AHEAD = 6
 QUANTISE_LAG = 1
 MULTIPLY_LAG = 2
-M_LEAD = PASSES - MULTIPLY_LAG
-M_LOAD_AT = PASSES - M_LEAD
+M_GROUP = 2
+M_ROUNDS = PASSES // M_GROUP
+VECTOR_BANK_EVERY = 8
 
 FLOPS = 2 * BATCH * IN_F * OUT_F + 2 * BATCH * RANK * OUT_F
 
@@ -73,7 +74,7 @@ def tile_lorasequential_pa_k_kernel(tc, x, h_lora, lora_B, M, out):
 
         def load_x(chunk):
             step, row_tile = divmod(chunk, ROW_TILES)
-            if row_tile == M_LOAD_AT and step + 1 < K_STEPS:
+            if row_tile == ROW_TILES - MULTIPLY_LAG and step + 1 < K_STEPS:
                 load_m(step + 1)
             raw = x_pool.tile([P, CHUNK_K], BF16, name="x_raw")
             x_rows = x[row_tile * P : (row_tile + 1) * P, step * CHUNK_K : (step + 1) * CHUNK_K]
@@ -83,52 +84,54 @@ def tile_lorasequential_pa_k_kernel(tc, x, h_lora, lora_B, M, out):
                 nc.sync.dma_start(out=raw[:, first : first + piece_k], in_=x_rows[:, first : first + piece_k])
             x_raw[chunk] = raw
 
-        def regroup_m(j):
-            step, g = divmod(j, PASSES)
-            grouped = m_grouped_pool.tile([P, OUT_F, PACK], BF16, name="m_grouped", align_bytes=64)
-            nc.vector.tensor_copy(out=grouped[:], in_=m_raw[step][:, g, :, :].rearrange("p t o -> p o t"))
-            m_grouped[j] = grouped
+        def regroup_m(step, j):
+            grouped = m_grouped_pool.tile([P, M_GROUP, OUT_F, PACK], BF16, name="m_grouped", align_bytes=64)
+            nc.vector.tensor_copy(
+                out=grouped[:],
+                in_=m_raw[step][:, j * M_GROUP : (j + 1) * M_GROUP, :, :].rearrange("p g t o -> p g o t"),
+            )
+            m_grouped[step, j] = grouped
 
-        def quantise_m(j):
-            step, g = divmod(j, PASSES)
-            if g == 0:
+        def quantise_m(step, j):
+            if j == 0:
                 m_codes[step] = m_mx_pool.tile([P, PASSES * OUT_F], U32, name="m_codes", align_bytes=64)
                 m_scales[step] = m_mx_pool.tile([P, PASSES * OUT_F], U8, name="m_scales", align_bytes=64)
-            cols = slice(g * OUT_F, (g + 1) * OUT_F)
+            cols = slice(j * M_GROUP * OUT_F, (j + 1) * M_GROUP * OUT_F)
             nc.vector.quantize_mx(
                 out=m_codes[step][:, cols].bitcast(FP8X4),
                 scales=m_scales[step][:, cols],
-                in_=m_grouped[j][:].rearrange("p o t -> p (o t)"),
+                in_=m_grouped[step, j][:].rearrange("p g o t -> p (g o t)"),
             )
 
         def transpose_x(chunk):
             words = x_raw[chunk][:].bitcast(F32)
             grouped = x_mx_pool.tile([P, PASSES * P * PACK], BF16, name="x_grouped", align_bytes=64)
             grouped_words = grouped[:].bitcast(F32)
-            bank_words = BANK_COLS // 2
+            bank_words = BANK_PASSES * P * 2
             for bank in range(CHUNK_BANKS):
                 xt = psum_t.tile([P, BANK_PASSES, 2, P], F32, name="xt", tag="bank")
                 for g in range(BANK_PASSES):
                     for u in range(2):
                         first = ((bank * BANK_PASSES + g) * 2 + u) * P
                         nc.tensor.transpose(xt[:, g, u, :], words[:, first : first + P], ident_f32[:])
-                nc.scalar.copy(
-                    out=grouped_words[:, bank * bank_words : (bank + 1) * bank_words].rearrange(
-                        "p (g r u) -> p g r u", g=BANK_PASSES, u=2
-                    ),
-                    in_=xt[:].rearrange("p g u r -> p g r u"),
+                side_by_side = grouped_words[:, bank * bank_words : (bank + 1) * bank_words].rearrange(
+                    "p (g r u) -> p g r u", g=BANK_PASSES, u=2
                 )
+                if (chunk * CHUNK_BANKS + bank) % VECTOR_BANK_EVERY == VECTOR_BANK_EVERY - 1:
+                    nc.vector.tensor_copy(out=side_by_side, in_=xt[:].rearrange("p g u r -> p g r u"))
+                else:
+                    nc.scalar.copy(out=side_by_side, in_=xt[:].rearrange("p g u r -> p g r u"))
             x_grouped[chunk] = grouped
 
         def quantise_x(chunk):
             codes = x_mx_pool.tile([P, PASSES * P], U32, name="x_codes", align_bytes=64)
             scales = x_mx_pool.tile([P, PASSES * P], U8, name="x_scales", align_bytes=64)
-            for first in range(0, CHUNK_BANKS * BANK_COLS, BANK_COLS):
-                cols = slice(first // PACK, (first + BANK_COLS) // PACK)
+            for first in range(0, PASSES * P * PACK, QUANT_COLS):
+                cols = slice(first // PACK, (first + QUANT_COLS) // PACK)
                 nc.vector.quantize_mx(
                     out=codes[:, cols].bitcast(FP8X4),
                     scales=scales[:, cols],
-                    in_=x_grouped[chunk][:, first : first + BANK_COLS],
+                    in_=x_grouped[chunk][:, first : first + QUANT_COLS],
                 )
             x_codes[chunk] = codes
             x_scales[chunk] = scales
@@ -155,19 +158,13 @@ def tile_lorasequential_pa_k_kernel(tc, x, h_lora, lora_B, M, out):
                 nc.vector.tensor_tensor(out=result[:], in0=acc[:], in1=sums[:, row_tile, :], op=ADD)
                 nc.sync.dma_start(out=out[row_tile * P : (row_tile + 1) * P, :], in_=result[:])
 
-        load_m(0)
         h_sb = const.tile([P, N_ADAPTERS, RANK], BF16)
         nc.sync.dma_start(out=h_sb[:], in_=h_lora.rearrange("g b r -> b g r"))
         b_sb = const.tile([P, N_ADAPTERS, OUT_F], BF16)
         nc.sync.dma_start(out=b_sb[:], in_=lora_B.rearrange("g r o -> r g o"))
+        load_m(0)
         for chunk in range(LOADS_AHEAD):
             load_x(chunk)
-
-        for j in range(PASSES):
-            regroup_m(j)
-            if j > 0:
-                quantise_m(j - 1)
-        quantise_m(PASSES - 1)
 
         sums = const.tile([P, ROW_TILES, OUT_F], F32)
         hT_ps = psum_t.tile([P, N_ADAPTERS, P], BF16, name="hT_ps", tag="bank")
@@ -184,18 +181,18 @@ def tile_lorasequential_pa_k_kernel(tc, x, h_lora, lora_B, M, out):
                 )
             nc.scalar.mul(out=sums[:, first : first + bank_groups, :], in_=y_ps[:], mul=LORA_GAIN)
 
-        for i in range(N_CHUNKS + MULTIPLY_LAG):
-            if i + LOADS_AHEAD < N_CHUNKS:
+        for i in range(-MULTIPLY_LAG, N_CHUNKS + MULTIPLY_LAG):
+            if 0 <= i and i + LOADS_AHEAD < N_CHUNKS:
                 load_x(i + LOADS_AHEAD)
-            if i >= MULTIPLY_LAG:
-                multiply(i - MULTIPLY_LAG)
-            if i < N_CHUNKS:
-                transpose_x(i)
-            m_pass = i + M_LEAD
-            prepare_m = PASSES <= m_pass < K_STEPS * PASSES
+            m_step, m_round = divmod(i + MULTIPLY_LAG, ROW_TILES)
+            prepare_m = m_step < K_STEPS and m_round < M_ROUNDS
             if prepare_m:
-                regroup_m(m_pass)
+                regroup_m(m_step, m_round)
             if 0 <= i - QUANTISE_LAG < N_CHUNKS:
                 quantise_x(i - QUANTISE_LAG)
             if prepare_m:
-                quantise_m(m_pass)
+                quantise_m(m_step, m_round)
+            if 0 <= i < N_CHUNKS:
+                transpose_x(i)
+            if i >= MULTIPLY_LAG:
+                multiply(i - MULTIPLY_LAG)

from contextlib import ExitStack

import concourse.mybir as mybir
from concourse.masks import make_identity

BF16 = mybir.dt.bfloat16
F32 = mybir.dt.float32
U32 = mybir.dt.uint32
U8 = mybir.dt.uint8
FP8X4 = mybir.dt.float8_e4m3fn_x4
ADD = mybir.AluOpType.add

P = 128
BATCH, IN_F, OUT_F, RANK, N_ADAPTERS = 1024, 16384, 128, 128, 8
LORA_GAIN = 2.0

PACK = 4
K_PASS = P * PACK
CHUNK_K = 4096
PASSES = CHUNK_K // K_PASS
K_STEPS = IN_F // CHUNK_K
ROW_TILES = BATCH // P
N_CHUNKS = K_STEPS * ROW_TILES
BANK_PASSES = 2
CHUNK_BANKS = PASSES // BANK_PASSES
QUANT_COLS = 2048

LOADS_AHEAD = 6
QUANTISE_LAG = 1
MULTIPLY_LAG = 2
M_GROUP = 2
M_ROUNDS = PASSES // M_GROUP
VECTOR_BANK_EVERY = 8

FLOPS = 2 * BATCH * IN_F * OUT_F + 2 * BATCH * RANK * OUT_F


def tile_lorasequential_pa_k_kernel(tc, x, h_lora, lora_B, M, out):
    nc = tc.nc
    with ExitStack() as ctx:
        ctx.enter_context(tc.manual_schedule())
        const = ctx.enter_context(tc.tile_pool(name="const", bufs=1))
        x_pool = ctx.enter_context(tc.tile_pool(name="x", bufs=LOADS_AHEAD + 1))
        x_mx_pool = ctx.enter_context(tc.tile_pool(name="x_mx", bufs=3))
        m_raw_pool = ctx.enter_context(tc.tile_pool(name="m_raw", bufs=2))
        m_grouped_pool = ctx.enter_context(tc.tile_pool(name="m_grouped", bufs=3))
        m_mx_pool = ctx.enter_context(tc.tile_pool(name="m_mx", bufs=2))
        result_pool = ctx.enter_context(tc.tile_pool(name="result", bufs=4))
        psum_t = ctx.enter_context(tc.psum_pool(name="psum_t", bufs=6))
        psum_acc = ctx.enter_context(tc.psum_pool(name="psum_acc", bufs=2))

        ident_f32 = const.tile([P, P], F32)
        make_identity(nc, ident_f32[:])
        ident_bf16 = const.tile([P, P], BF16)
        make_identity(nc, ident_bf16[:])

        x_raw = {}
        x_grouped = {}
        x_codes = {}
        x_scales = {}
        m_raw = {}
        m_grouped = {}
        m_codes = {}
        m_scales = {}

        def load_m(step):
            raw = m_raw_pool.tile([P, PASSES, PACK, OUT_F], BF16, name="m_raw")
            m_rows = M[step * CHUNK_K : (step + 1) * CHUNK_K, :]
            nc.sync.dma_start(
                out=raw[:].rearrange("p g (u e) o -> p g u e o", u=2),
                in_=m_rows.rearrange("(g u p e) o -> p g u e o", u=2, p=P, e=2),
            )
            m_raw[step] = raw

        def load_x(chunk):
            step, row_tile = divmod(chunk, ROW_TILES)
            if row_tile == ROW_TILES - MULTIPLY_LAG and step + 1 < K_STEPS:
                load_m(step + 1)
            raw = x_pool.tile([P, CHUNK_K], BF16, name="x_raw")
            x_rows = x[row_tile * P : (row_tile + 1) * P, step * CHUNK_K : (step + 1) * CHUNK_K]
            pieces = CHUNK_BANKS if chunk == N_CHUNKS - 1 else 1
            piece_k = CHUNK_K // pieces
            for first in range(0, CHUNK_K, piece_k):
                nc.sync.dma_start(out=raw[:, first : first + piece_k], in_=x_rows[:, first : first + piece_k])
            x_raw[chunk] = raw

        def regroup_m(step, j):
            grouped = m_grouped_pool.tile([P, M_GROUP, OUT_F, PACK], BF16, name="m_grouped", align_bytes=64)
            nc.vector.tensor_copy(
                out=grouped[:],
                in_=m_raw[step][:, j * M_GROUP : (j + 1) * M_GROUP, :, :].rearrange("p g t o -> p g o t"),
            )
            m_grouped[step, j] = grouped

        def quantise_m(step, j):
            if j == 0:
                m_codes[step] = m_mx_pool.tile([P, PASSES * OUT_F], U32, name="m_codes", align_bytes=64)
                m_scales[step] = m_mx_pool.tile([P, PASSES * OUT_F], U8, name="m_scales", align_bytes=64)
            cols = slice(j * M_GROUP * OUT_F, (j + 1) * M_GROUP * OUT_F)
            nc.vector.quantize_mx(
                out=m_codes[step][:, cols].bitcast(FP8X4),
                scales=m_scales[step][:, cols],
                in_=m_grouped[step, j][:].rearrange("p g o t -> p (g o t)"),
            )

        def transpose_x(chunk):
            words = x_raw[chunk][:].bitcast(F32)
            grouped = x_mx_pool.tile([P, PASSES * P * PACK], BF16, name="x_grouped", align_bytes=64)
            grouped_words = grouped[:].bitcast(F32)
            bank_words = BANK_PASSES * P * 2
            for bank in range(CHUNK_BANKS):
                xt = psum_t.tile([P, BANK_PASSES, 2, P], F32, name="xt", tag="bank")
                for g in range(BANK_PASSES):
                    for u in range(2):
                        first = ((bank * BANK_PASSES + g) * 2 + u) * P
                        nc.tensor.transpose(xt[:, g, u, :], words[:, first : first + P], ident_f32[:])
                side_by_side = grouped_words[:, bank * bank_words : (bank + 1) * bank_words].rearrange(
                    "p (g r u) -> p g r u", g=BANK_PASSES, u=2
                )
                if (chunk * CHUNK_BANKS + bank) % VECTOR_BANK_EVERY == VECTOR_BANK_EVERY - 1:
                    nc.vector.tensor_copy(out=side_by_side, in_=xt[:].rearrange("p g u r -> p g r u"))
                else:
                    nc.scalar.copy(out=side_by_side, in_=xt[:].rearrange("p g u r -> p g r u"))
            x_grouped[chunk] = grouped

        def quantise_x(chunk):
            codes = x_mx_pool.tile([P, PASSES * P], U32, name="x_codes", align_bytes=64)
            scales = x_mx_pool.tile([P, PASSES * P], U8, name="x_scales", align_bytes=64)
            for first in range(0, PASSES * P * PACK, QUANT_COLS):
                cols = slice(first // PACK, (first + QUANT_COLS) // PACK)
                nc.vector.quantize_mx(
                    out=codes[:, cols].bitcast(FP8X4),
                    scales=scales[:, cols],
                    in_=x_grouped[chunk][:, first : first + QUANT_COLS],
                )
            x_codes[chunk] = codes
            x_scales[chunk] = scales

        def multiply(chunk):
            step, row_tile = divmod(chunk, ROW_TILES)
            acc = psum_acc.tile([P, OUT_F], F32, name="acc")
            for g in range(PASSES):
                rows = slice(g * P, (g + 1) * P)
                outputs = slice(g * OUT_F, (g + 1) * OUT_F)
                nc.tensor.matmul_mx(
                    out=acc[:],
                    lhsT=x_codes[chunk][:, rows].bitcast(FP8X4),
                    lhsT_scale=x_scales[chunk][:, rows],
                    rhs=m_codes[step][:, outputs].bitcast(FP8X4),
                    rhs_scale=m_scales[step][:, outputs],
                    start=(g == 0),
                    stop=(g == PASSES - 1),
                )
            if step < K_STEPS - 1:
                nc.vector.tensor_tensor(out=sums[:, row_tile, :], in0=acc[:], in1=sums[:, row_tile, :], op=ADD)
            else:
                result = result_pool.tile([P, OUT_F], F32, name="result")
                nc.vector.tensor_tensor(out=result[:], in0=acc[:], in1=sums[:, row_tile, :], op=ADD)
                nc.sync.dma_start(out=out[row_tile * P : (row_tile + 1) * P, :], in_=result[:])

        h_sb = const.tile([P, N_ADAPTERS, RANK], BF16)
        nc.sync.dma_start(out=h_sb[:], in_=h_lora.rearrange("g b r -> b g r"))
        b_sb = const.tile([P, N_ADAPTERS, OUT_F], BF16)
        nc.sync.dma_start(out=b_sb[:], in_=lora_B.rearrange("g r o -> r g o"))
        load_m(0)
        for chunk in range(LOADS_AHEAD):
            load_x(chunk)

        sums = const.tile([P, ROW_TILES, OUT_F], F32)
        hT_ps = psum_t.tile([P, N_ADAPTERS, P], BF16, name="hT_ps", tag="bank")
        for g in range(N_ADAPTERS):
            nc.tensor.transpose(hT_ps[:, g, :], h_sb[:, g, :], ident_bf16[:])
        hT_sb = const.tile([P, N_ADAPTERS, P], BF16)
        nc.scalar.copy(out=hT_sb[:], in_=hT_ps[:])
        bank_groups = 4
        for first in range(0, N_ADAPTERS, bank_groups):
            y_ps = psum_t.tile([P, bank_groups, OUT_F], F32, name="y_ps", tag="bank")
            for g in range(bank_groups):
                nc.tensor.matmul(
                    y_ps[:, g, :], lhsT=hT_sb[:, first + g, :], rhs=b_sb[:, first + g, :], start=True, stop=True
                )
            nc.scalar.mul(out=sums[:, first : first + bank_groups, :], in_=y_ps[:], mul=LORA_GAIN)

        for i in range(-MULTIPLY_LAG, N_CHUNKS + MULTIPLY_LAG):
            if 0 <= i and i + LOADS_AHEAD < N_CHUNKS:
                load_x(i + LOADS_AHEAD)
            m_step, m_round = divmod(i + MULTIPLY_LAG, ROW_TILES)
            prepare_m = m_step < K_STEPS and m_round < M_ROUNDS
            if prepare_m:
                regroup_m(m_step, m_round)
            if 0 <= i - QUANTISE_LAG < N_CHUNKS:
                quantise_x(i - QUANTISE_LAG)
            if prepare_m:
                quantise_m(m_step, m_round)
            if 0 <= i < N_CHUNKS:
                transpose_x(i)
            if i >= MULTIPLY_LAG:
                multiply(i - MULTIPLY_LAG)
